import numpy as np
import ml_dtypes

BF16 = ml_dtypes.bfloat16


def bf(x):
    return np.asarray(x, np.float32).astype(BF16)


def f32(x):
    return np.asarray(x, np.float32)


def f64(x):
    return np.asarray(x).astype(np.float64)


def striped(idx):
    return np.tile(idx.reshape(-1, 16).T, (8, 1))


S, D, KN, HL, NP, N = 256, 128, 4, 128, 8, 1024


def setup_inputs():
    idx = np.concatenate([np.random.permutation(S)[:HL] for _ in range(NP)])
    return {
        "table": bf(np.random.standard_normal((S, D))),
        "xq": bf(np.random.standard_normal((D, S))),
        "wq": bf(np.random.standard_normal((D, D)) / np.sqrt(D)),
        "bq": f32(0.1 * np.random.standard_normal((D, 1))),
        "wk": bf(np.random.standard_normal((D, D)) / np.sqrt(D)),
        "wv": bf(np.random.standard_normal((D, D)) / np.sqrt(D)),
        "bv": f32(0.1 * np.random.standard_normal((D, 1))),
        "offs": striped(idx),
    }


def reference(table, xq, wq, bq, wk, wv, bv, offs):
    idx = offs[:16].T.reshape(-1)
    q = f64(wq).T @ f64(xq) + f64(bq)
    picked = f64(table)[idx].T
    key = (f64(wk).T @ picked).reshape(D, KN, S)
    val = (f64(wv).T @ picked + f64(bv)).reshape(D, KN, S)
    s = (q[:, None, :] * key).sum(axis=0) / np.sqrt(D)
    e = np.exp(s - s.max(axis=0, keepdims=True))
    a = e / e.sum(axis=0, keepdims=True)
    return q + (a[None, :, :] * val).sum(axis=1)

@@ -1,0 +1,110 @@
+import math
+
+import concourse.mybir as mybir
+from concourse.masks import make_identity
+
+S, D, KN, N = 256, 128, 4, 1024
+P = 128
+BANK = 512
+BF16, F32, U16 = mybir.dt.bfloat16, mybir.dt.float32, mybir.dt.uint16
+ACT = mybir.ActivationFunctionType
+ALU = mybir.AluOpType
+
+FLOPS = 2 * D * D * (S + 2 * N) + 4 * D * N
+
+
+def tile_multiscaleknngraphattention_kernel(tc, table, xq, wq, bq, wk, wv, bv, offs, out):
+    nc = tc.nc
+    with tc.tile_pool(name="held", bufs=1) as held, tc.psum_pool(name="banks", bufs=1) as banks:
+        offsets = held.tile([P, N // 16], U16, name="offsets")
+        nc.sync.dma_start(offsets[:], offs)
+        table_rows = held.tile([P, S // P, D], BF16, name="table_rows")
+        nc.scalar.dma_start(table_rows[:], table.rearrange("(b p) d -> p b d", p=P))
+        wk_sb = held.tile([D, D], BF16, name="wk_sb")
+        nc.sync.dma_start(wk_sb[:], wk)
+        xq_sb = held.tile([D, S], BF16, name="xq_sb")
+        nc.scalar.dma_start(xq_sb[:], xq)
+        wq_sb = held.tile([D, D], BF16, name="wq_sb")
+        nc.sync.dma_start(wq_sb[:], wq)
+        wv_sb = held.tile([D, D], BF16, name="wv_sb")
+        nc.scalar.dma_start(wv_sb[:], wv)
+        bq_sb = held.tile([D, 1], F32, name="bq_sb")
+        nc.sync.dma_start(bq_sb[:], bq)
+        bv_sb = held.tile([D, 1], F32, name="bv_sb")
+        nc.scalar.dma_start(bv_sb[:], bv)
+
+        identity = held.tile([P, P], BF16, name="identity")
+        make_identity(nc, identity[:])
+        ones = held.tile([D, P], BF16, name="ones")
+        nc.vector.memset(ones[:], 1.0)
+
+        flipped = banks.tile([D, S], BF16, name="flipped")
+        for b in range(S // P):
+            nc.tensor.transpose(flipped[:, b * P : (b + 1) * P], table_rows[:, b, :], identity[:])
+        window = held.tile([D, S], BF16, name="window")
+        nc.vector.tensor_copy(window[:], flipped[:])
+
+        q_ps = banks.tile([D, S], F32, name="q_ps")
+        nc.tensor.matmul(q_ps[:], wq_sb[:], xq_sb[:], start=True, stop=True)
+        q_sb = held.tile([D, S], F32, name="q_sb")
+        nc.scalar.activation(q_sb[:], q_ps[:], ACT.Identity, bias=bq_sb[:])
+        q_twice = q_sb[:].unsqueeze(1).to_broadcast([D, BANK // S, S])
+
+        key_ps = [banks.tile([D, BANK], F32, name=f"key_ps{b}") for b in range(N // BANK)]
+        val_ps = [banks.tile([D, BANK], F32, name=f"val_ps{b}") for b in range(N // BANK)]
+        for weights, product in ((wk_sb, key_ps), (wv_sb, val_ps)):
+            for r in range(KN):
+                looked_up = window[:].indirect(offsets[:, r * (S // 16) : (r + 1) * (S // 16)])
+                column = (r * S) % BANK
+                nc.tensor.matmul(
+                    product[r * S // BANK][:, column : column + S], weights[:], looked_up, start=True, stop=True
+                )
+
+        prod = held.tile([D, N], BF16, name="prod")
+        s_ps = [banks.tile([P, BANK], F32, name=f"s_ps{b}") for b in range(N // BANK)]
+        for b in range(N // BANK):
+            nc.vector.tensor_tensor(
+                prod[:, b * BANK : (b + 1) * BANK].rearrange("p (r n) -> p r n", n=S),
+                key_ps[b][:].rearrange("p (r n) -> p r n", n=S),
+                q_twice,
+                ALU.mult,
+            )
+            nc.tensor.matmul(s_ps[b][:], ones[:], prod[:, b * BANK : (b + 1) * BANK], start=True, stop=True)
+
+        top_of_bank = held.tile([P, N // BANK, S], F32, name="top_of_bank")
+        for b in range(N // BANK):
+            nc.vector.tensor_reduce(
+                top_of_bank[:, b, :], s_ps[b][:].rearrange("p (r n) -> p n r", n=S), mybir.AxisListType.X, ALU.max
+            )
+        top = held.tile([P, S], F32, name="top")
+        nc.vector.tensor_max(top[:], top_of_bank[:, 0, :], top_of_bank[:, 1, :])
+        top_twice = top[:].unsqueeze(1).to_broadcast([P, BANK // S, S])
+        below = held.tile([P, N], F32, name="below")
+        e = held.tile([P, N], F32, name="e")
+        ev = held.tile([P, N], F32, name="ev")
+        for b in range(N // BANK):
+            half = slice(b * BANK, (b + 1) * BANK)
+            nc.vector.tensor_tensor(
+                below[:, half].rearrange("p (r n) -> p r n", n=S),
+                s_ps[b][:].rearrange("p (r n) -> p r n", n=S),
+                top_twice,
+                ALU.subtract,
+            )
+            nc.scalar.activation(e[:, half], below[:, half], ACT.Exp, scale=1.0 / math.sqrt(D))
+            nc.vector.tensor_mul(ev[:, half], e[:, half], val_ps[b][:])
+
+        e2 = held.tile([P, BANK], F32, name="e2")
+        nc.vector.tensor_add(e2[:], e[:, :BANK], e[:, BANK:])
+        e1 = held.tile([P, S], F32, name="e1")
+        nc.vector.tensor_add(e1[:], e2[:, :S], e2[:, S:])
+        inverse = held.tile([P, S], F32, name="inverse")
+        nc.vector.reciprocal(inverse[:], e1[:])
+        ev2 = held.tile([P, BANK], F32, name="ev2")
+        nc.vector.tensor_add(ev2[:], ev[:, :BANK], ev[:, BANK:])
+        ev1 = held.tile([P, S], F32, name="ev1")
+        nc.vector.tensor_add(ev1[:], ev2[:, :S], ev2[:, S:])
+        mixed = held.tile([P, S], F32, name="mixed")
+        nc.vector.tensor_mul(mixed[:], ev1[:], inverse[:])
+        result = held.tile([P, S], F32, name="result")
+        nc.vector.scalar_tensor_tensor(result[:], mixed[:], bv_sb[:], q_sb[:], ALU.add, ALU.add)
+        nc.sync.dma_start(out, result[:])

@@ -6,9 +6,12 @@ from concourse.masks import make_identity
 S, D, KN, N = 256, 128, 4, 1024
 P = 128
 BANK = 512
+HALVES = S // P
+BLOCKS = N // P
 BF16, F32, U16 = mybir.dt.bfloat16, mybir.dt.float32, mybir.dt.uint16
 ACT = mybir.ActivationFunctionType
 ALU = mybir.AluOpType
+X = mybir.AxisListType.X
 
 FLOPS = 2 * D * D * (S + 2 * N) + 4 * D * N
 
@@ -18,7 +21,7 @@ def tile_multiscaleknngraphattention_kernel(tc, table, xq, wq, bq, wk, wv, bv, o
     with tc.tile_pool(name="held", bufs=1) as held, tc.psum_pool(name="banks", bufs=1) as banks:
         offsets = held.tile([P, N // 16], U16, name="offsets")
         nc.sync.dma_start(offsets[:], offs)
-        table_rows = held.tile([P, S // P, D], BF16, name="table_rows")
+        table_rows = held.tile([P, HALVES, D], BF16, name="table_rows")
         nc.scalar.dma_start(table_rows[:], table.rearrange("(b p) d -> p b d", p=P))
         wk_sb = held.tile([D, D], BF16, name="wk_sb")
         nc.sync.dma_start(wk_sb[:], wk)
@@ -26,21 +29,26 @@ def tile_multiscaleknngraphattention_kernel(tc, table, xq, wq, bq, wk, wv, bv, o
         nc.scalar.dma_start(xq_sb[:], xq)
         wq_sb = held.tile([D, D], BF16, name="wq_sb")
         nc.sync.dma_start(wq_sb[:], wq)
-        wv_sb = held.tile([D, D], BF16, name="wv_sb")
-        nc.scalar.dma_start(wv_sb[:], wv)
         bq_sb = held.tile([D, 1], F32, name="bq_sb")
-        nc.sync.dma_start(bq_sb[:], bq)
+        nc.scalar.dma_start(bq_sb[:], bq)
+        wv_sb = held.tile([D, D], BF16, name="wv_sb")
+        nc.sync.dma_start(wv_sb[:], wv)
         bv_sb = held.tile([D, 1], F32, name="bv_sb")
         nc.scalar.dma_start(bv_sb[:], bv)
 
-        identity = held.tile([P, P], BF16, name="identity")
-        make_identity(nc, identity[:])
-        ones = held.tile([D, P], BF16, name="ones")
+        identity_bf = held.tile([P, P], BF16, name="identity_bf")
+        make_identity(nc, identity_bf[:])
+        identity_f = held.tile([P, P], F32, name="identity_f")
+        make_identity(nc, identity_f[:])
+        ones = held.tile([D, 1], BF16, name="ones")
         nc.vector.memset(ones[:], 1.0)
+        warm = held.tile([P, 1], F32, name="warm")
+        nc.vector.memset(warm[:], 0.0)
+        nc.scalar.activation(warm[:], warm[:], ACT.Exp)
 
-        flipped = banks.tile([D, S], BF16, name="flipped")
-        for b in range(S // P):
-            nc.tensor.transpose(flipped[:, b * P : (b + 1) * P], table_rows[:, b, :], identity[:])
+        flipped = banks.tile([D, S], BF16, name="flipped", tag="narrow")
+        for b in range(HALVES):
+            nc.tensor.transpose(flipped[:, b * P : (b + 1) * P], table_rows[:, b, :], identity_bf[:])
         window = held.tile([D, S], BF16, name="window")
         nc.vector.tensor_copy(window[:], flipped[:])
 
@@ -61,7 +69,6 @@ def tile_multiscaleknngraphattention_kernel(tc, table, xq, wq, bq, wk, wv, bv, o
                 )
 
         prod = held.tile([D, N], BF16, name="prod")
-        s_ps = [banks.tile([P, BANK], F32, name=f"s_ps{b}") for b in range(N // BANK)]
         for b in range(N // BANK):
             nc.vector.tensor_tensor(
                 prod[:, b * BANK : (b + 1) * BANK].rearrange("p (r n) -> p r n", n=S),
@@ -69,42 +76,56 @@ def tile_multiscaleknngraphattention_kernel(tc, table, xq, wq, bq, wk, wv, bv, o
                 q_twice,
                 ALU.mult,
             )
-            nc.tensor.matmul(s_ps[b][:], ones[:], prod[:, b * BANK : (b + 1) * BANK], start=True, stop=True)
+        score = banks.tile([P, BLOCKS], F32, name="score", tag="narrow")
+        for t in range(BLOCKS):
+            nc.tensor.matmul(score[:, t : t + 1], prod[:, t * P : (t + 1) * P], ones[:], start=True, stop=True)
 
-        top_of_bank = held.tile([P, N // BANK, S], F32, name="top_of_bank")
+        val_sb = held.tile([D, N], F32, name="val_sb")
         for b in range(N // BANK):
-            nc.vector.tensor_reduce(
-                top_of_bank[:, b, :], s_ps[b][:].rearrange("p (r n) -> p n r", n=S), mybir.AxisListType.X, ALU.max
-            )
-        top = held.tile([P, S], F32, name="top")
-        nc.vector.tensor_max(top[:], top_of_bank[:, 0, :], top_of_bank[:, 1, :])
-        top_twice = top[:].unsqueeze(1).to_broadcast([P, BANK // S, S])
-        below = held.tile([P, N], F32, name="below")
-        e = held.tile([P, N], F32, name="e")
-        ev = held.tile([P, N], F32, name="ev")
-        for b in range(N // BANK):
-            half = slice(b * BANK, (b + 1) * BANK)
+            nc.scalar.activation(val_sb[:, b * BANK : (b + 1) * BANK], val_ps[b][:], ACT.Identity, bias=bv_sb[:])
+
+        top = held.tile([P, HALVES], F32, name="top")
+        nc.vector.tensor_reduce(top[:], score[:].rearrange("p (r h) -> p h r", h=HALVES), X, ALU.max)
+        below = held.tile([P, BLOCKS], F32, name="below")
+        nc.vector.tensor_tensor(
+            below[:].rearrange("p (r h) -> p r h", h=HALVES),
+            score[:].rearrange("p (r h) -> p r h", h=HALVES),
+            top[:].unsqueeze(1).to_broadcast([P, KN, HALVES]),
+            ALU.subtract,
+        )
+        e = held.tile([P, BLOCKS], F32, name="e")
+        nc.scalar.activation(e[:], below[:], ACT.Exp, scale=1.0 / math.sqrt(D))
+        total = held.tile([P, HALVES], F32, name="total")
+        nc.vector.tensor_reduce(total[:], e[:].rearrange("p (r h) -> p h r", h=HALVES), X, ALU.add)
+        inverse = held.tile([P, HALVES], F32, name="inverse")
+        nc.vector.reciprocal(inverse[:], total[:])
+        a = held.tile([P, BLOCKS], F32, name="a")
+        nc.vector.tensor_tensor(
+            a[:].rearrange("p (r h) -> p r h", h=HALVES),
+            e[:].rearrange("p (r h) -> p r h", h=HALVES),
+            inverse[:].unsqueeze(1).to_broadcast([P, KN, HALVES]),
+            ALU.mult,
+        )
+
+        result = held.tile([D, S], F32, name="result")
+        for h in range(HALVES):
+            a_ps = banks.tile([P, KN * P], F32, name=f"a_ps{h}", tag=f"key_ps{h}")
+            for r in range(KN):
+                t = HALVES * r + h
+                nc.tensor.transpose(
+                    a_ps[:, r * P : (r + 1) * P], a[:, t : t + 1].to_broadcast([P, P]), identity_f[:]
+                )
+            av = held.tile([D, KN * P], F32, name=f"av{h}")
             nc.vector.tensor_tensor(
-                below[:, half].rearrange("p (r n) -> p r n", n=S),
-                s_ps[b][:].rearrange("p (r n) -> p r n", n=S),
-                top_twice,
-                ALU.subtract,
+                av[:].rearrange("p (r n) -> p r n", n=P),
+                a_ps[:].rearrange("p (r n) -> p r n", n=P),
+                val_sb[:].rearrange("p (r h n) -> p h r n", h=HALVES, n=P)[:, h],
+                ALU.mult,
             )
-            nc.scalar.activation(e[:, half], below[:, half], ACT.Exp, scale=1.0 / math.sqrt(D))
-            nc.vector.tensor_mul(ev[:, half], e[:, half], val_ps[b][:])
-
-        e2 = held.tile([P, BANK], F32, name="e2")
-        nc.vector.tensor_add(e2[:], e[:, :BANK], e[:, BANK:])
-        e1 = held.tile([P, S], F32, name="e1")
-        nc.vector.tensor_add(e1[:], e2[:, :S], e2[:, S:])
-        inverse = held.tile([P, S], F32, name="inverse")
-        nc.vector.reciprocal(inverse[:], e1[:])
-        ev2 = held.tile([P, BANK], F32, name="ev2")
-        nc.vector.tensor_add(ev2[:], ev[:, :BANK], ev[:, BANK:])
-        ev1 = held.tile([P, S], F32, name="ev1")
-        nc.vector.tensor_add(ev1[:], ev2[:, :S], ev2[:, S:])
-        mixed = held.tile([P, S], F32, name="mixed")
-        nc.vector.tensor_mul(mixed[:], ev1[:], inverse[:])
-        result = held.tile([P, S], F32, name="result")
-        nc.vector.scalar_tensor_tensor(result[:], mixed[:], bv_sb[:], q_sb[:], ALU.add, ALU.add)
-        nc.sync.dma_start(out, result[:])
+            av2 = held.tile([D, 2 * P], F32, name=f"av2{h}")
+            nc.vector.tensor_add(av2[:], av[:, : 2 * P], av[:, 2 * P :])
+            av1 = held.tile([D, P], F32, name=f"av1{h}")
+            nc.vector.tensor_add(av1[:], av2[:, :P], av2[:, P:])
+            nodes = slice(h * P, (h + 1) * P)
+            nc.vector.tensor_add(result[:, nodes], av1[:], q_sb[:, nodes])
+            (nc.sync, nc.scalar)[h].dma_start(out[:, nodes], result[:, nodes])

@@ -7,7 +7,6 @@ S, D, KN, N = 256, 128, 4, 1024
 P = 128
 BANK = 512
 HALVES = S // P
-BLOCKS = N // P
 BF16, F32, U16 = mybir.dt.bfloat16, mybir.dt.float32, mybir.dt.uint16
 ACT = mybir.ActivationFunctionType
 ALU = mybir.AluOpType
@@ -40,11 +39,20 @@ def tile_multiscaleknngraphattention_kernel(tc, table, xq, wq, bq, wk, wv, bv, o
         make_identity(nc, identity_bf[:])
         identity_f = held.tile([P, P], F32, name="identity_f")
         make_identity(nc, identity_f[:])
-        ones = held.tile([D, 1], BF16, name="ones")
-        nc.vector.memset(ones[:], 1.0)
         warm = held.tile([P, 1], F32, name="warm")
         nc.vector.memset(warm[:], 0.0)
         nc.scalar.activation(warm[:], warm[:], ACT.Exp)
+        same = held.tile([D, KN, KN], BF16, name="same")
+        nc.gpsimd.memset(same[:], 0.0)
+        for b in range(KN):
+            nc.gpsimd.memset(same[:, b, b : b + 1], 1.0)
+        signs = held.tile([D, KN, KN, KN], BF16, name="signs")
+        nc.vector.tensor_tensor(
+            signs[:],
+            same[:].unsqueeze(2).to_broadcast([D, KN, KN, KN]),
+            same[:].unsqueeze(3).to_broadcast([D, KN, KN, KN]),
+            ALU.subtract,
+        )
 
         flipped = banks.tile([D, S], BF16, name="flipped", tag="narrow")
         for b in range(HALVES):
@@ -52,80 +60,56 @@ def tile_multiscaleknngraphattention_kernel(tc, table, xq, wq, bq, wk, wv, bv, o
         window = held.tile([D, S], BF16, name="window")
         nc.vector.tensor_copy(window[:], flipped[:])
 
+        terms = held.tile([D, KN + 1, S], F32, name="terms")
+        q = terms[:, KN, :]
         q_ps = banks.tile([D, S], F32, name="q_ps")
         nc.tensor.matmul(q_ps[:], wq_sb[:], xq_sb[:], start=True, stop=True)
-        q_sb = held.tile([D, S], F32, name="q_sb")
-        nc.scalar.activation(q_sb[:], q_ps[:], ACT.Identity, bias=bq_sb[:])
-        q_twice = q_sb[:].unsqueeze(1).to_broadcast([D, BANK // S, S])
+        nc.scalar.activation(q, q_ps[:], ACT.Identity, bias=bq_sb[:])
 
-        key_ps = [banks.tile([D, BANK], F32, name=f"key_ps{b}") for b in range(N // BANK)]
-        val_ps = [banks.tile([D, BANK], F32, name=f"val_ps{b}") for b in range(N // BANK)]
+        key_ps = [banks.tile([D, BANK // S, S], F32, name=f"key_ps{b}") for b in range(N // BANK)]
+        val_ps = [banks.tile([D, BANK // S, S], F32, name=f"val_ps{b}") for b in range(N // BANK)]
         for weights, product in ((wk_sb, key_ps), (wv_sb, val_ps)):
             for r in range(KN):
                 looked_up = window[:].indirect(offsets[:, r * (S // 16) : (r + 1) * (S // 16)])
-                column = (r * S) % BANK
                 nc.tensor.matmul(
-                    product[r * S // BANK][:, column : column + S], weights[:], looked_up, start=True, stop=True
+                    product[r * S // BANK][:, r % (BANK // S), :], weights[:], looked_up, start=True, stop=True
                 )
-
-        prod = held.tile([D, N], BF16, name="prod")
+        prod = held.tile([D, KN, S], BF16, name="prod")
         for b in range(N // BANK):
+            ranks = slice(b * BANK // S, (b + 1) * BANK // S)
             nc.vector.tensor_tensor(
-                prod[:, b * BANK : (b + 1) * BANK].rearrange("p (r n) -> p r n", n=S),
-                key_ps[b][:].rearrange("p (r n) -> p r n", n=S),
-                q_twice,
-                ALU.mult,
+                prod[:, ranks, :], key_ps[b][:], q.unsqueeze(1).to_broadcast([D, BANK // S, S]), ALU.mult
             )
-        score = banks.tile([P, BLOCKS], F32, name="score", tag="narrow")
-        for t in range(BLOCKS):
-            nc.tensor.matmul(score[:, t : t + 1], prod[:, t * P : (t + 1) * P], ones[:], start=True, stop=True)
 
-        val_sb = held.tile([D, N], F32, name="val_sb")
+        diff = banks.tile([P, HALVES, KN, KN], F32, name="diff", tag="narrow")
+        for h in range(HALVES):
+            for b in range(KN):
+                nc.tensor.matmul(
+                    diff[:, h], prod[:, b, h * P : (h + 1) * P], signs[:, b], start=(b == 0), stop=(b == KN - 1)
+                )
+        spare = banks.tile([P, BANK], F32, name="spare", tag="key_ps0")
         for b in range(N // BANK):
-            nc.scalar.activation(val_sb[:, b * BANK : (b + 1) * BANK], val_ps[b][:], ACT.Identity, bias=bv_sb[:])
+            nc.tensor.matmul(spare[:], identity_bf[:], prod[:, b * BANK // S : (b + 1) * BANK // S, :], start=True, stop=True)
 
-        top = held.tile([P, HALVES], F32, name="top")
-        nc.vector.tensor_reduce(top[:], score[:].rearrange("p (r h) -> p h r", h=HALVES), X, ALU.max)
-        below = held.tile([P, BLOCKS], F32, name="below")
-        nc.vector.tensor_tensor(
-            below[:].rearrange("p (r h) -> p r h", h=HALVES),
-            score[:].rearrange("p (r h) -> p r h", h=HALVES),
-            top[:].unsqueeze(1).to_broadcast([P, KN, HALVES]),
-            ALU.subtract,
-        )
-        e = held.tile([P, BLOCKS], F32, name="e")
-        nc.scalar.activation(e[:], below[:], ACT.Exp, scale=1.0 / math.sqrt(D))
-        total = held.tile([P, HALVES], F32, name="total")
-        nc.vector.tensor_reduce(total[:], e[:].rearrange("p (r h) -> p h r", h=HALVES), X, ALU.add)
-        inverse = held.tile([P, HALVES], F32, name="inverse")
-        nc.vector.reciprocal(inverse[:], total[:])
-        a = held.tile([P, BLOCKS], F32, name="a")
-        nc.vector.tensor_tensor(
-            a[:].rearrange("p (r h) -> p r h", h=HALVES),
-            e[:].rearrange("p (r h) -> p r h", h=HALVES),
-            inverse[:].unsqueeze(1).to_broadcast([P, KN, HALVES]),
-            ALU.mult,
-        )
+        e = held.tile([P, HALVES * KN, KN], F32, name="e")
+        nc.scalar.activation(e[:], diff[:].rearrange("p h r x -> p (h r) x"), ACT.Exp, scale=1.0 / math.sqrt(D))
+        val_sb = held.tile([D, KN, S], F32, name="val_sb")
+        nc.vector.tensor_scalar(val_sb[:, 0 : BANK // S, :], val_ps[0][:], bv_sb[:], None, ALU.add)
+        nc.scalar.activation(val_sb[:, BANK // S : KN, :], val_ps[1][:], ACT.Identity, bias=bv_sb[:])
+        total = held.tile([P, HALVES * KN], F32, name="total")
+        nc.vector.tensor_reduce(total[:], e[:], X, ALU.add)
+        a = held.tile([P, HALVES * KN], F32, name="a")
+        nc.vector.reciprocal(a[:], total[:])
 
+        for h in range(HALVES):
+            a_ps = banks.tile([P, KN, P], F32, name=f"a_ps{h}")
+            for r in range(KN):
+                column = h * KN + r
+                nc.tensor.transpose(a_ps[:, r, :], a[:, column : column + 1].to_broadcast([P, P]), identity_f[:])
+            nodes = slice(h * P, (h + 1) * P)
+            nc.vector.tensor_tensor(terms[:, 0:KN, nodes], a_ps[:], val_sb[:, :, nodes], ALU.mult)
         result = held.tile([D, S], F32, name="result")
         for h in range(HALVES):
-            a_ps = banks.tile([P, KN * P], F32, name=f"a_ps{h}", tag=f"key_ps{h}")
-            for r in range(KN):
-                t = HALVES * r + h
-                nc.tensor.transpose(
-                    a_ps[:, r * P : (r + 1) * P], a[:, t : t + 1].to_broadcast([P, P]), identity_f[:]
-                )
-            av = held.tile([D, KN * P], F32, name=f"av{h}")
-            nc.vector.tensor_tensor(
-                av[:].rearrange("p (r n) -> p r n", n=P),
-                a_ps[:].rearrange("p (r n) -> p r n", n=P),
-                val_sb[:].rearrange("p (r h n) -> p h r n", h=HALVES, n=P)[:, h],
-                ALU.mult,
-            )
-            av2 = held.tile([D, 2 * P], F32, name=f"av2{h}")
-            nc.vector.tensor_add(av2[:], av[:, : 2 * P], av[:, 2 * P :])
-            av1 = held.tile([D, P], F32, name=f"av1{h}")
-            nc.vector.tensor_add(av1[:], av2[:, :P], av2[:, P:])
             nodes = slice(h * P, (h + 1) * P)
-            nc.vector.tensor_add(result[:, nodes], av1[:], q_sb[:, nodes])
+            nc.vector.tensor_reduce(result[:, nodes], terms[:, :, nodes].rearrange("p r n -> p n r"), X, ALU.add)
             (nc.sync, nc.scalar)[h].dma_start(out[:, nodes], result[:, nodes])

@@ -60,11 +60,11 @@ def tile_multiscaleknngraphattention_kernel(tc, table, xq, wq, bq, wk, wv, bv, o
         window = held.tile([D, S], BF16, name="window")
         nc.vector.tensor_copy(window[:], flipped[:])
 
-        terms = held.tile([D, KN + 1, S], F32, name="terms")
-        q = terms[:, KN, :]
         q_ps = banks.tile([D, S], F32, name="q_ps")
         nc.tensor.matmul(q_ps[:], wq_sb[:], xq_sb[:], start=True, stop=True)
-        nc.scalar.activation(q, q_ps[:], ACT.Identity, bias=bq_sb[:])
+        q_sb = held.tile([D, S], F32, name="q_sb")
+        nc.scalar.activation(q_sb[:], q_ps[:], ACT.Identity, bias=bq_sb[:])
+        q_twice = q_sb[:].unsqueeze(1).to_broadcast([D, BANK // S, S])
 
         key_ps = [banks.tile([D, BANK // S, S], F32, name=f"key_ps{b}") for b in range(N // BANK)]
         val_ps = [banks.tile([D, BANK // S, S], F32, name=f"val_ps{b}") for b in range(N // BANK)]
@@ -77,9 +77,7 @@ def tile_multiscaleknngraphattention_kernel(tc, table, xq, wq, bq, wk, wv, bv, o
         prod = held.tile([D, KN, S], BF16, name="prod")
         for b in range(N // BANK):
             ranks = slice(b * BANK // S, (b + 1) * BANK // S)
-            nc.vector.tensor_tensor(
-                prod[:, ranks, :], key_ps[b][:], q.unsqueeze(1).to_broadcast([D, BANK // S, S]), ALU.mult
-            )
+            nc.vector.tensor_tensor(prod[:, ranks, :], key_ps[b][:], q_twice, ALU.mult)
 
         diff = banks.tile([P, HALVES, KN, KN], F32, name="diff", tag="narrow")
         for h in range(HALVES):
@@ -93,23 +91,32 @@ def tile_multiscaleknngraphattention_kernel(tc, table, xq, wq, bq, wk, wv, bv, o
 
         e = held.tile([P, HALVES * KN, KN], F32, name="e")
         nc.scalar.activation(e[:], diff[:].rearrange("p h r x -> p (h r) x"), ACT.Exp, scale=1.0 / math.sqrt(D))
-        val_sb = held.tile([D, KN, S], F32, name="val_sb")
-        nc.vector.tensor_scalar(val_sb[:, 0 : BANK // S, :], val_ps[0][:], bv_sb[:], None, ALU.add)
-        nc.scalar.activation(val_sb[:, BANK // S : KN, :], val_ps[1][:], ACT.Identity, bias=bv_sb[:])
         total = held.tile([P, HALVES * KN], F32, name="total")
-        nc.vector.tensor_reduce(total[:], e[:], X, ALU.add)
         a = held.tile([P, HALVES * KN], F32, name="a")
-        nc.vector.reciprocal(a[:], total[:])
 
-        for h in range(HALVES):
+        val_sb = held.tile([D, KN, S], F32, name="val_sb")
+
+        def values_leave(b):
+            ranks = slice(b * BANK // S, (b + 1) * BANK // S)
+            nc.vector.scalar_tensor_tensor(val_sb[:, ranks, :], val_ps[b][:], bv_sb[:], q_twice, ALU.add, ALU.add)
+
+        values_leave(0)
+        nc.vector.tensor_reduce(total[:], e[:], X, ALU.add)
+        nc.vector.reciprocal(a[:], total[:])
+        values_leave(1)
+
+        halves = [slice(h * P, (h + 1) * P) for h in range(HALVES)]
+        weighted = held.tile([D, KN, S], F32, name="weighted")
+        for h, nodes in enumerate(halves):
             a_ps = banks.tile([P, KN, P], F32, name=f"a_ps{h}")
             for r in range(KN):
                 column = h * KN + r
                 nc.tensor.transpose(a_ps[:, r, :], a[:, column : column + 1].to_broadcast([P, P]), identity_f[:])
-            nodes = slice(h * P, (h + 1) * P)
-            nc.vector.tensor_tensor(terms[:, 0:KN, nodes], a_ps[:], val_sb[:, :, nodes], ALU.mult)
+            nc.vector.tensor_tensor(weighted[:, :, nodes], a_ps[:], val_sb[:, :, nodes], ALU.mult)
+        pairs = held.tile([D, KN // 2, S], F32, name="pairs")
+        for nodes in halves:
+            nc.vector.tensor_add(pairs[:, :, nodes], weighted[:, 0 : KN // 2, nodes], weighted[:, KN // 2 : KN, nodes])
         result = held.tile([D, S], F32, name="result")
-        for h in range(HALVES):
-            nodes = slice(h * P, (h + 1) * P)
-            nc.vector.tensor_reduce(result[:, nodes], terms[:, :, nodes].rearrange("p r n -> p n r"), X, ALU.add)
+        for h, nodes in enumerate(halves):
+            nc.vector.tensor_add(result[:, nodes], pairs[:, 0, nodes], pairs[:, 1, nodes])
             (nc.sync, nc.scalar)[h].dma_start(out[:, nodes], result[:, nodes])

@@ -7,6 +7,7 @@ S, D, KN, N = 256, 128, 4, 1024
 P = 128
 BANK = 512
 HALVES = S // P
+PAIR = S // P
 BF16, F32, U16 = mybir.dt.bfloat16, mybir.dt.float32, mybir.dt.uint16
 ACT = mybir.ActivationFunctionType
 ALU = mybir.AluOpType
@@ -17,11 +18,14 @@ FLOPS = 2 * D * D * (S + 2 * N) + 4 * D * N
 
 def tile_multiscaleknngraphattention_kernel(tc, table, xq, wq, bq, wk, wv, bv, offs, out):
     nc = tc.nc
-    with tc.tile_pool(name="held", bufs=1) as held, tc.psum_pool(name="banks", bufs=1) as banks:
+    with tc.tile_pool(name="held", bufs=1) as held, tc.psum_pool(name="banks", bufs=8) as banks:
+        def bank(name, shape, dtype):
+            return banks.tile(shape, dtype, name=name, tag="bank")
+
         offsets = held.tile([P, N // 16], U16, name="offsets")
         nc.sync.dma_start(offsets[:], offs)
-        table_rows = held.tile([P, HALVES, D], BF16, name="table_rows")
-        nc.scalar.dma_start(table_rows[:], table.rearrange("(b p) d -> p b d", p=P))
+        table_rows = held.tile([P, PAIR, D], BF16, name="table_rows")
+        nc.scalar.dma_start(table_rows[:], table.rearrange("(p i) d -> p i d", i=PAIR))
         wk_sb = held.tile([D, D], BF16, name="wk_sb")
         nc.sync.dma_start(wk_sb[:], wk)
         xq_sb = held.tile([D, S], BF16, name="xq_sb")
@@ -54,20 +58,25 @@ def tile_multiscaleknngraphattention_kernel(tc, table, xq, wq, bq, wk, wv, bv, o
             ALU.subtract,
         )
 
-        flipped = banks.tile([D, S], BF16, name="flipped", tag="narrow")
-        for b in range(HALVES):
-            nc.tensor.transpose(flipped[:, b * P : (b + 1) * P], table_rows[:, b, :], identity_bf[:])
-        window = held.tile([D, S], BF16, name="window")
-        nc.vector.tensor_copy(window[:], flipped[:])
+        bias_out = held.tile([D, 1], F32, name="bias_out")
+        nc.gpsimd.tensor_tensor(bias_out[:], bq_sb[:], bv_sb[:], ALU.add)
 
-        q_ps = banks.tile([D, S], F32, name="q_ps")
+        halves = [slice(h * P, (h + 1) * P) for h in range(HALVES)]
+
+        flipped = bank("flipped", [D, PAIR, P], BF16)
+        for i in range(PAIR):
+            nc.tensor.transpose(flipped[:, i, :], table_rows[:, i, :], identity_bf[:])
+        window = held.tile([D, S], BF16, name="window")
+        nc.vector.tensor_copy(window[:].rearrange("d (p i) -> d p i", i=PAIR), flipped[:].rearrange("d i p -> d p i"))
+
+        q_ps = bank("q_ps", [D, S], F32)
         nc.tensor.matmul(q_ps[:], wq_sb[:], xq_sb[:], start=True, stop=True)
         q_sb = held.tile([D, S], F32, name="q_sb")
         nc.scalar.activation(q_sb[:], q_ps[:], ACT.Identity, bias=bq_sb[:])
         q_twice = q_sb[:].unsqueeze(1).to_broadcast([D, BANK // S, S])
 
-        key_ps = [banks.tile([D, BANK // S, S], F32, name=f"key_ps{b}") for b in range(N // BANK)]
-        val_ps = [banks.tile([D, BANK // S, S], F32, name=f"val_ps{b}") for b in range(N // BANK)]
+        key_ps = [bank(f"key_ps{b}", [D, BANK // S, S], F32) for b in range(N // BANK)]
+        val_ps = [bank(f"val_ps{b}", [D, BANK // S, S], F32) for b in range(N // BANK)]
         for weights, product in ((wk_sb, key_ps), (wv_sb, val_ps)):
             for r in range(KN):
                 looked_up = window[:].indirect(offsets[:, r * (S // 16) : (r + 1) * (S // 16)])
@@ -79,44 +88,41 @@ def tile_multiscaleknngraphattention_kernel(tc, table, xq, wq, bq, wk, wv, bv, o
             ranks = slice(b * BANK // S, (b + 1) * BANK // S)
             nc.vector.tensor_tensor(prod[:, ranks, :], key_ps[b][:], q_twice, ALU.mult)
 
-        diff = banks.tile([P, HALVES, KN, KN], F32, name="diff", tag="narrow")
-        for h in range(HALVES):
+        diff = bank("diff", [P, HALVES, KN, KN], F32)
+        for h, nodes in enumerate(halves):
             for b in range(KN):
-                nc.tensor.matmul(
-                    diff[:, h], prod[:, b, h * P : (h + 1) * P], signs[:, b], start=(b == 0), stop=(b == KN - 1)
-                )
-        spare = banks.tile([P, BANK], F32, name="spare", tag="key_ps0")
-        for b in range(N // BANK):
-            nc.tensor.matmul(spare[:], identity_bf[:], prod[:, b * BANK // S : (b + 1) * BANK // S, :], start=True, stop=True)
+                nc.tensor.matmul(diff[:, h], prod[:, b, nodes], signs[:, b], start=(b == 0), stop=(b == KN - 1))
+
+        out_ps = [bank(f"out_ps{h}", [D, P], F32) for h in range(HALVES)]
+        for h, nodes in enumerate(halves):
+            nc.tensor.matmul(out_ps[h][:], wq_sb[:], xq_sb[:, nodes], start=True, stop=False)
+
+        val_sb = held.tile([D, KN, S], F32, name="val_sb")
+        nc.scalar.copy(val_sb[:, 0 : BANK // S, :], val_ps[0][:])
+        nc.vector.tensor_copy(val_sb[:, BANK // S : KN, :], val_ps[1][:])
+        valT_ps = [bank(f"valT_ps{r}", [P, HALVES, D], F32) for r in range(KN)]
+        for r in range(KN):
+            for h, nodes in enumerate(halves):
+                nc.tensor.transpose(valT_ps[r][:, h, :], val_sb[:, r, nodes], identity_f[:])
 
         e = held.tile([P, HALVES * KN, KN], F32, name="e")
         nc.scalar.activation(e[:], diff[:].rearrange("p h r x -> p (h r) x"), ACT.Exp, scale=1.0 / math.sqrt(D))
         total = held.tile([P, HALVES * KN], F32, name="total")
-        a = held.tile([P, HALVES * KN], F32, name="a")
-
-        val_sb = held.tile([D, KN, S], F32, name="val_sb")
-
-        def values_leave(b):
-            ranks = slice(b * BANK // S, (b + 1) * BANK // S)
-            nc.vector.scalar_tensor_tensor(val_sb[:, ranks, :], val_ps[b][:], bv_sb[:], q_twice, ALU.add, ALU.add)
-
-        values_leave(0)
         nc.vector.tensor_reduce(total[:], e[:], X, ALU.add)
+        a = held.tile([P, HALVES * KN], F32, name="a")
         nc.vector.reciprocal(a[:], total[:])
-        values_leave(1)
 
-        halves = [slice(h * P, (h + 1) * P) for h in range(HALVES)]
-        weighted = held.tile([D, KN, S], F32, name="weighted")
-        for h, nodes in enumerate(halves):
-            a_ps = banks.tile([P, KN, P], F32, name=f"a_ps{h}")
-            for r in range(KN):
-                column = h * KN + r
-                nc.tensor.transpose(a_ps[:, r, :], a[:, column : column + 1].to_broadcast([P, P]), identity_f[:])
-            nc.vector.tensor_tensor(weighted[:, :, nodes], a_ps[:], val_sb[:, :, nodes], ALU.mult)
-        pairs = held.tile([D, KN // 2, S], F32, name="pairs")
-        for nodes in halves:
-            nc.vector.tensor_add(pairs[:, :, nodes], weighted[:, 0 : KN // 2, nodes], weighted[:, KN // 2 : KN, nodes])
+        scaled = held.tile([P, KN, HALVES, D], F32, name="scaled")
+        for r in range(KN):
+            nc.vector.tensor_scalar(scaled[:, r, 0, :], valT_ps[r][:, 0, :], a[:, r : r + 1], None, ALU.mult)
+            nc.scalar.activation(scaled[:, r, 1, :], valT_ps[r][:, 1, :], ACT.Copy, scale=a[:, KN + r : KN + r + 1])
+            for h in range(HALVES):
+                nc.tensor.matmul(
+                    out_ps[h][:], scaled[:, r, h, :], identity_f[:], is_transpose=True, start=False, stop=(r == KN - 1)
+                )
+
         result = held.tile([D, S], F32, name="result")
-        for h, nodes in enumerate(halves):
-            nc.vector.tensor_add(result[:, nodes], pairs[:, 0, nodes], pairs[:, 1, nodes])
-            (nc.sync, nc.scalar)[h].dma_start(out[:, nodes], result[:, nodes])
+        nc.vector.tensor_scalar(result[:, halves[0]], out_ps[0][:], bias_out[:], None, ALU.add)
+        nc.sync.dma_start(out[:, halves[0]], result[:, halves[0]])
+        nc.scalar.activation(result[:, halves[1]], out_ps[1][:], ACT.Identity, bias=bias_out[:])
+        nc.scalar.dma_start(out[:, halves[1]], result[:, halves[1]])

@@ -7,7 +7,6 @@ S, D, KN, N = 256, 128, 4, 1024
 P = 128
 BANK = 512
 HALVES = S // P
-PAIR = S // P
 BF16, F32, U16 = mybir.dt.bfloat16, mybir.dt.float32, mybir.dt.uint16
 ACT = mybir.ActivationFunctionType
 ALU = mybir.AluOpType
@@ -24,8 +23,8 @@ def tile_multiscaleknngraphattention_kernel(tc, table, xq, wq, bq, wk, wv, bv, o
 
         offsets = held.tile([P, N // 16], U16, name="offsets")
         nc.sync.dma_start(offsets[:], offs)
-        table_rows = held.tile([P, PAIR, D], BF16, name="table_rows")
-        nc.scalar.dma_start(table_rows[:], table.rearrange("(p i) d -> p i d", i=PAIR))
+        table_rows = held.tile([P, HALVES, D], BF16, name="table_rows")
+        nc.scalar.dma_start(table_rows[:], table.rearrange("(h p) d -> p h d", p=P))
         wk_sb = held.tile([D, D], BF16, name="wk_sb")
         nc.sync.dma_start(wk_sb[:], wk)
         xq_sb = held.tile([D, S], BF16, name="xq_sb")
@@ -63,17 +62,21 @@ def tile_multiscaleknngraphattention_kernel(tc, table, xq, wq, bq, wk, wv, bv, o
 
         halves = [slice(h * P, (h + 1) * P) for h in range(HALVES)]
 
-        flipped = bank("flipped", [D, PAIR, P], BF16)
-        for i in range(PAIR):
-            nc.tensor.transpose(flipped[:, i, :], table_rows[:, i, :], identity_bf[:])
+        flipped = bank("flipped", [D, S], BF16)
+        for h, nodes in enumerate(halves):
+            nc.tensor.transpose(flipped[:, nodes], table_rows[:, h, :], identity_bf[:])
         window = held.tile([D, S], BF16, name="window")
-        nc.vector.tensor_copy(window[:].rearrange("d (p i) -> d p i", i=PAIR), flipped[:].rearrange("d i p -> d p i"))
+        nc.vector.tensor_copy(window[:], flipped[:])
 
         q_ps = bank("q_ps", [D, S], F32)
         nc.tensor.matmul(q_ps[:], wq_sb[:], xq_sb[:], start=True, stop=True)
         q_sb = held.tile([D, S], F32, name="q_sb")
         nc.scalar.activation(q_sb[:], q_ps[:], ACT.Identity, bias=bq_sb[:])
         q_twice = q_sb[:].unsqueeze(1).to_broadcast([D, BANK // S, S])
+
+        out_ps = [bank(f"out_ps{h}", [D, P], F32) for h in range(HALVES)]
+        for h, nodes in enumerate(halves):
+            nc.tensor.matmul(out_ps[h][:], wq_sb[:], xq_sb[:, nodes], start=True, stop=False)
 
         key_ps = [bank(f"key_ps{b}", [D, BANK // S, S], F32) for b in range(N // BANK)]
         val_ps = [bank(f"val_ps{b}", [D, BANK // S, S], F32) for b in range(N // BANK)]
@@ -93,10 +96,6 @@ def tile_multiscaleknngraphattention_kernel(tc, table, xq, wq, bq, wk, wv, bv, o
             for b in range(KN):
                 nc.tensor.matmul(diff[:, h], prod[:, b, nodes], signs[:, b], start=(b == 0), stop=(b == KN - 1))
 
-        out_ps = [bank(f"out_ps{h}", [D, P], F32) for h in range(HALVES)]
-        for h, nodes in enumerate(halves):
-            nc.tensor.matmul(out_ps[h][:], wq_sb[:], xq_sb[:, nodes], start=True, stop=False)
-
         val_sb = held.tile([D, KN, S], F32, name="val_sb")
         nc.scalar.copy(val_sb[:, 0 : BANK // S, :], val_ps[0][:])
         nc.vector.tensor_copy(val_sb[:, BANK // S : KN, :], val_ps[1][:])
@@ -112,13 +111,24 @@ def tile_multiscaleknngraphattention_kernel(tc, table, xq, wq, bq, wk, wv, bv, o
         a = held.tile([P, HALVES * KN], F32, name="a")
         nc.vector.reciprocal(a[:], total[:])
 
-        scaled = held.tile([P, KN, HALVES, D], F32, name="scaled")
-        for r in range(KN):
-            nc.vector.tensor_scalar(scaled[:, r, 0, :], valT_ps[r][:, 0, :], a[:, r : r + 1], None, ALU.mult)
-            nc.scalar.activation(scaled[:, r, 1, :], valT_ps[r][:, 1, :], ACT.Copy, scale=a[:, KN + r : KN + r + 1])
+        odd = held.tile([P, KN // 2, HALVES, D], F32, name="odd")
+        both = held.tile([P, KN // 2, HALVES, D], F32, name="both")
+        for k in range(KN // 2):
             for h in range(HALVES):
+                even_column, odd_column = h * KN + 2 * k, h * KN + 2 * k + 1
+                nc.scalar.activation(
+                    odd[:, k, h, :], valT_ps[2 * k + 1][:, h, :], ACT.Copy, scale=a[:, odd_column : odd_column + 1]
+                )
+                nc.vector.scalar_tensor_tensor(
+                    both[:, k, h, :],
+                    valT_ps[2 * k][:, h, :],
+                    a[:, even_column : even_column + 1],
+                    odd[:, k, h, :],
+                    ALU.mult,
+                    ALU.add,
+                )
                 nc.tensor.matmul(
-                    out_ps[h][:], scaled[:, r, h, :], identity_f[:], is_transpose=True, start=False, stop=(r == KN - 1)
+                    out_ps[h][:], both[:, k, h, :], identity_f[:], is_transpose=True, start=False, stop=(k == KN // 2 - 1)
                 )
 
         result = held.tile([D, S], F32, name="result")

@@ -7,6 +7,7 @@ S, D, KN, N = 256, 128, 4, 1024
 P = 128
 BANK = 512
 HALVES = S // P
+WARM_UP = 5
 BF16, F32, U16 = mybir.dt.bfloat16, mybir.dt.float32, mybir.dt.uint16
 ACT = mybir.ActivationFunctionType
 ALU = mybir.AluOpType
@@ -37,6 +38,14 @@ def tile_multiscaleknngraphattention_kernel(tc, table, xq, wq, bq, wk, wv, bv, o
         nc.sync.dma_start(wv_sb[:], wv)
         bv_sb = held.tile([D, 1], F32, name="bv_sb")
         nc.scalar.dma_start(bv_sb[:], bv)
+
+        nothing = held.tile([P, 1], BF16, name="nothing")
+        nc.gpsimd.memset(nothing[:], 0.0)
+        idle_ps = bank("idle_ps", [P, BANK], F32)
+        for i in range(WARM_UP):
+            nc.tensor.matmul(
+                idle_ps[:], nothing[:].to_broadcast([P, P]), nothing[:].to_broadcast([P, BANK]), start=True, stop=True
+            )
 
         identity_bf = held.tile([P, P], BF16, name="identity_bf")
         make_identity(nc, identity_bf[:])

@@ -120,25 +120,18 @@ def tile_multiscaleknngraphattention_kernel(tc, table, xq, wq, bq, wk, wv, bv, o
         a = held.tile([P, HALVES * KN], F32, name="a")
         nc.vector.reciprocal(a[:], total[:])
 
-        odd = held.tile([P, KN // 2, HALVES, D], F32, name="odd")
-        both = held.tile([P, KN // 2, HALVES, D], F32, name="both")
+        scaled = held.tile([P, KN, HALVES, D], F32, name="scaled")
         for k in range(KN // 2):
             for h in range(HALVES):
-                even_column, odd_column = h * KN + 2 * k, h * KN + 2 * k + 1
-                nc.scalar.activation(
-                    odd[:, k, h, :], valT_ps[2 * k + 1][:, h, :], ACT.Copy, scale=a[:, odd_column : odd_column + 1]
-                )
-                nc.vector.scalar_tensor_tensor(
-                    both[:, k, h, :],
-                    valT_ps[2 * k][:, h, :],
-                    a[:, even_column : even_column + 1],
-                    odd[:, k, h, :],
-                    ALU.mult,
-                    ALU.add,
-                )
-                nc.tensor.matmul(
-                    out_ps[h][:], both[:, k, h, :], identity_f[:], is_transpose=True, start=False, stop=(k == KN // 2 - 1)
-                )
+                for r in (2 * k, 2 * k + 1):
+                    column = a[:, h * KN + r : h * KN + r + 1]
+                    if r % 2 == 0:
+                        nc.vector.tensor_scalar(scaled[:, r, h, :], valT_ps[r][:, h, :], column, None, ALU.mult)
+                    else:
+                        nc.scalar.activation(scaled[:, r, h, :], valT_ps[r][:, h, :], ACT.Copy, scale=column)
+                    nc.tensor.matmul(
+                        out_ps[h][:], scaled[:, r, h, :], identity_f[:], is_transpose=True, start=False, stop=(r == KN - 1)
+                    )
 
         result = held.tile([D, S], F32, name="result")
         nc.vector.tensor_scalar(result[:, halves[0]], out_ps[0][:], bias_out[:], None, ALU.add)

@@ -137,4 +137,4 @@ def tile_multiscaleknngraphattention_kernel(tc, table, xq, wq, bq, wk, wv, bv, o
         nc.vector.tensor_scalar(result[:, halves[0]], out_ps[0][:], bias_out[:], None, ALU.add)
         nc.sync.dma_start(out[:, halves[0]], result[:, halves[0]])
         nc.scalar.activation(result[:, halves[1]], out_ps[1][:], ACT.Identity, bias=bias_out[:])
-        nc.scalar.dma_start(out[:, halves[1]], result[:, halves[1]])
+        nc.sync.dma_start(out[:, halves[1]], result[:, halves[1]])

@@ -22,22 +22,22 @@ def tile_multiscaleknngraphattention_kernel(tc, table, xq, wq, bq, wk, wv, bv, o
         def bank(name, shape, dtype):
             return banks.tile(shape, dtype, name=name, tag="bank")
 
+        table_rows = held.tile([P, HALVES, D], BF16, name="table_rows")
+        nc.sync.dma_start(table_rows[:], table.rearrange("(h p) d -> p h d", p=P))
         offsets = held.tile([P, N // 16], U16, name="offsets")
         nc.sync.dma_start(offsets[:], offs)
-        table_rows = held.tile([P, HALVES, D], BF16, name="table_rows")
-        nc.scalar.dma_start(table_rows[:], table.rearrange("(h p) d -> p h d", p=P))
         wk_sb = held.tile([D, D], BF16, name="wk_sb")
         nc.sync.dma_start(wk_sb[:], wk)
         xq_sb = held.tile([D, S], BF16, name="xq_sb")
-        nc.scalar.dma_start(xq_sb[:], xq)
+        nc.sync.dma_start(xq_sb[:], xq)
         wq_sb = held.tile([D, D], BF16, name="wq_sb")
         nc.sync.dma_start(wq_sb[:], wq)
         bq_sb = held.tile([D, 1], F32, name="bq_sb")
-        nc.scalar.dma_start(bq_sb[:], bq)
+        nc.sync.dma_start(bq_sb[:], bq)
         wv_sb = held.tile([D, D], BF16, name="wv_sb")
         nc.sync.dma_start(wv_sb[:], wv)
         bv_sb = held.tile([D, 1], F32, name="bv_sb")
-        nc.scalar.dma_start(bv_sb[:], bv)
+        nc.sync.dma_start(bv_sb[:], bv)
 
         nothing = held.tile([P, 1], BF16, name="nothing")
         nc.gpsimd.memset(nothing[:], 0.0)

@@ -55,9 +55,9 @@ def tile_multiscaleknngraphattention_kernel(tc, table, xq, wq, bq, wk, wv, bv, o
         nc.vector.memset(warm[:], 0.0)
         nc.scalar.activation(warm[:], warm[:], ACT.Exp)
         same = held.tile([D, KN, KN], BF16, name="same")
-        nc.gpsimd.memset(same[:], 0.0)
+        nc.vector.memset(same[:], 0.0)
         for b in range(KN):
-            nc.gpsimd.memset(same[:, b, b : b + 1], 1.0)
+            nc.vector.memset(same[:, b, b : b + 1], 1.0)
         signs = held.tile([D, KN, KN, KN], BF16, name="signs")
         nc.vector.tensor_tensor(
             signs[:],
@@ -65,9 +65,6 @@ def tile_multiscaleknngraphattention_kernel(tc, table, xq, wq, bq, wk, wv, bv, o
             same[:].unsqueeze(3).to_broadcast([D, KN, KN, KN]),
             ALU.subtract,
         )
-
-        bias_out = held.tile([D, 1], F32, name="bias_out")
-        nc.gpsimd.tensor_tensor(bias_out[:], bq_sb[:], bv_sb[:], ALU.add)
 
         halves = [slice(h * P, (h + 1) * P) for h in range(HALVES)]
 
@@ -133,6 +130,8 @@ def tile_multiscaleknngraphattention_kernel(tc, table, xq, wq, bq, wk, wv, bv, o
                         out_ps[h][:], scaled[:, r, h, :], identity_f[:], is_transpose=True, start=False, stop=(r == KN - 1)
                     )
 
+        bias_out = held.tile([D, 1], F32, name="bias_out")
+        nc.gpsimd.tensor_tensor(bias_out[:], bq_sb[:], bv_sb[:], ALU.add)
         result = held.tile([D, S], F32, name="result")
         nc.vector.tensor_scalar(result[:, halves[0]], out_ps[0][:], bias_out[:], None, ALU.add)
         nc.sync.dma_start(out[:, halves[0]], result[:, halves[0]])

@@ -7,7 +7,7 @@ S, D, KN, N = 256, 128, 4, 1024
 P = 128
 BANK = 512
 HALVES = S // P
-WARM_UP = 5
+WARM_UP = 4
 BF16, F32, U16 = mybir.dt.bfloat16, mybir.dt.float32, mybir.dt.uint16
 ACT = mybir.ActivationFunctionType
 ALU = mybir.AluOpType

@@ -24,14 +24,14 @@ def tile_multiscaleknngraphattention_kernel(tc, table, xq, wq, bq, wk, wv, bv, o
 
         table_rows = held.tile([P, HALVES, D], BF16, name="table_rows")
         nc.sync.dma_start(table_rows[:], table.rearrange("(h p) d -> p h d", p=P))
-        offsets = held.tile([P, N // 16], U16, name="offsets")
-        nc.sync.dma_start(offsets[:], offs)
-        wk_sb = held.tile([D, D], BF16, name="wk_sb")
-        nc.sync.dma_start(wk_sb[:], wk)
         xq_sb = held.tile([D, S], BF16, name="xq_sb")
         nc.sync.dma_start(xq_sb[:], xq)
         wq_sb = held.tile([D, D], BF16, name="wq_sb")
         nc.sync.dma_start(wq_sb[:], wq)
+        offsets = held.tile([P, N // 16], U16, name="offsets")
+        nc.sync.dma_start(offsets[:], offs)
+        wk_sb = held.tile([D, D], BF16, name="wk_sb")
+        nc.sync.dma_start(wk_sb[:], wk)
         bq_sb = held.tile([D, 1], F32, name="bq_sb")
         nc.sync.dma_start(bq_sb[:], bq)
         wv_sb = held.tile([D, D], BF16, name="wv_sb")
@@ -80,10 +80,6 @@ def tile_multiscaleknngraphattention_kernel(tc, table, xq, wq, bq, wk, wv, bv, o
         nc.scalar.activation(q_sb[:], q_ps[:], ACT.Identity, bias=bq_sb[:])
         q_twice = q_sb[:].unsqueeze(1).to_broadcast([D, BANK // S, S])
 
-        out_ps = [bank(f"out_ps{h}", [D, P], F32) for h in range(HALVES)]
-        for h, nodes in enumerate(halves):
-            nc.tensor.matmul(out_ps[h][:], wq_sb[:], xq_sb[:, nodes], start=True, stop=False)
-
         key_ps = [bank(f"key_ps{b}", [D, BANK // S, S], F32) for b in range(N // BANK)]
         val_ps = [bank(f"val_ps{b}", [D, BANK // S, S], F32) for b in range(N // BANK)]
         for weights, product in ((wk_sb, key_ps), (wv_sb, val_ps)):
@@ -109,6 +105,10 @@ def tile_multiscaleknngraphattention_kernel(tc, table, xq, wq, bq, wk, wv, bv, o
         for r in range(KN):
             for h, nodes in enumerate(halves):
                 nc.tensor.transpose(valT_ps[r][:, h, :], val_sb[:, r, nodes], identity_f[:])
+
+        out_ps = [bank(f"out_ps{h}", [D, P], F32) for h in range(HALVES)]
+        for h, nodes in enumerate(halves):
+            nc.tensor.matmul(out_ps[h][:], wq_sb[:], xq_sb[:, nodes], start=True, stop=False)
 
         e = held.tile([P, HALVES * KN, KN], F32, name="e")
         nc.scalar.activation(e[:], diff[:].rearrange("p h r x -> p (h r) x"), ACT.Exp, scale=1.0 / math.sqrt(D))

@@ -98,6 +98,9 @@ def tile_multiscaleknngraphattention_kernel(tc, table, xq, wq, bq, wk, wv, bv, o
             for b in range(KN):
                 nc.tensor.matmul(diff[:, h], prod[:, b, nodes], signs[:, b], start=(b == 0), stop=(b == KN - 1))
 
+        idle_ps = bank("idle_ps", [P, BANK], F32)
+        nc.tensor.matmul(idle_ps[:], prod[:, KN - 1, halves[1]], prod[:, KN - 2 : KN, :], start=True, stop=True)
+
         val_sb = held.tile([D, KN, S], F32, name="val_sb")
         nc.scalar.copy(val_sb[:, 0 : BANK // S, :], val_ps[0][:])
         nc.vector.tensor_copy(val_sb[:, BANK // S : KN, :], val_ps[1][:])
@@ -105,6 +108,8 @@ def tile_multiscaleknngraphattention_kernel(tc, table, xq, wq, bq, wk, wv, bv, o
         for r in range(KN):
             for h, nodes in enumerate(halves):
                 nc.tensor.transpose(valT_ps[r][:, h, :], val_sb[:, r, nodes], identity_f[:])
+
+        nc.tensor.matmul(idle_ps[:, 0:P], identity_f[:], val_sb[:, KN - 1, halves[1]], start=True, stop=True)
 
         out_ps = [bank(f"out_ps{h}", [D, P], F32) for h in range(HALVES)]
         for h, nodes in enumerate(halves):

@@ -7,7 +7,7 @@ S, D, KN, N = 256, 128, 4, 1024
 P = 128
 BANK = 512
 HALVES = S // P
-WARM_UP = 4
+WARM_UP = 3
 BF16, F32, U16 = mybir.dt.bfloat16, mybir.dt.float32, mybir.dt.uint16
 ACT = mybir.ActivationFunctionType
 ALU = mybir.AluOpType

@@ -7,7 +7,7 @@ S, D, KN, N = 256, 128, 4, 1024
 P = 128
 BANK = 512
 HALVES = S // P
-WARM_UP = 3
+WARM_UP = 7
 BF16, F32, U16 = mybir.dt.bfloat16, mybir.dt.float32, mybir.dt.uint16
 ACT = mybir.ActivationFunctionType
 ALU = mybir.AluOpType
@@ -44,7 +44,11 @@ def tile_multiscaleknngraphattention_kernel(tc, table, xq, wq, bq, wk, wv, bv, o
         idle_ps = bank("idle_ps", [P, BANK], F32)
         for i in range(WARM_UP):
             nc.tensor.matmul(
-                idle_ps[:], nothing[:].to_broadcast([P, P]), nothing[:].to_broadcast([P, BANK]), start=True, stop=True
+                idle_ps[:, 0 : BANK // 2],
+                nothing[:].to_broadcast([P, P]),
+                nothing[:].to_broadcast([P, BANK // 2]),
+                start=True,
+                stop=True,
             )
 
         identity_bf = held.tile([P, P], BF16, name="identity_bf")
@@ -80,6 +84,10 @@ def tile_multiscaleknngraphattention_kernel(tc, table, xq, wq, bq, wk, wv, bv, o
         nc.scalar.activation(q_sb[:], q_ps[:], ACT.Identity, bias=bq_sb[:])
         q_twice = q_sb[:].unsqueeze(1).to_broadcast([D, BANK // S, S])
 
+        out_ps = [bank(f"out_ps{h}", [D, P], F32) for h in range(HALVES)]
+        for h, nodes in enumerate(halves):
+            nc.tensor.matmul(out_ps[h][:], wq_sb[:], xq_sb[:, nodes], start=True, stop=False)
+
         key_ps = [bank(f"key_ps{b}", [D, BANK // S, S], F32) for b in range(N // BANK)]
         val_ps = [bank(f"val_ps{b}", [D, BANK // S, S], F32) for b in range(N // BANK)]
         for weights, product in ((wk_sb, key_ps), (wv_sb, val_ps)):
@@ -110,10 +118,6 @@ def tile_multiscaleknngraphattention_kernel(tc, table, xq, wq, bq, wk, wv, bv, o
                 nc.tensor.transpose(valT_ps[r][:, h, :], val_sb[:, r, nodes], identity_f[:])
 
         nc.tensor.matmul(idle_ps[:, 0:P], identity_f[:], val_sb[:, KN - 1, halves[1]], start=True, stop=True)
-
-        out_ps = [bank(f"out_ps{h}", [D, P], F32) for h in range(HALVES)]
-        for h, nodes in enumerate(halves):
-            nc.tensor.matmul(out_ps[h][:], wq_sb[:], xq_sb[:, nodes], start=True, stop=False)
 
         e = held.tile([P, HALVES * KN, KN], F32, name="e")
         nc.scalar.activation(e[:], diff[:].rearrange("p h r x -> p (h r) x"), ACT.Exp, scale=1.0 / math.sqrt(D))

@@ -54,7 +54,7 @@ def tile_multiscaleknngraphattention_kernel(tc, table, xq, wq, bq, wk, wv, bv, o
         identity_bf = held.tile([P, P], BF16, name="identity_bf")
         make_identity(nc, identity_bf[:])
         identity_f = held.tile([P, P], F32, name="identity_f")
-        make_identity(nc, identity_f[:])
+        nc.vector.tensor_copy(identity_f[:], identity_bf[:])
         warm = held.tile([P, 1], F32, name="warm")
         nc.vector.memset(warm[:], 0.0)
         nc.scalar.activation(warm[:], warm[:], ACT.Exp)
@@ -89,13 +89,15 @@ def tile_multiscaleknngraphattention_kernel(tc, table, xq, wq, bq, wk, wv, bv, o
             nc.tensor.matmul(out_ps[h][:], wq_sb[:], xq_sb[:, nodes], start=True, stop=False)
 
         key_ps = [bank(f"key_ps{b}", [D, BANK // S, S], F32) for b in range(N // BANK)]
-        val_ps = [bank(f"val_ps{b}", [D, BANK // S, S], F32) for b in range(N // BANK)]
-        for weights, product in ((wk_sb, key_ps), (wv_sb, val_ps)):
+        val_01 = bank("val_01", [D, BANK // S, S], F32)
+        val_2 = bank("val_2", [D, S], F32)
+        val_3 = bank("val_3", [D, S], F32)
+        keys = [key_ps[r * S // BANK][:, r % (BANK // S), :] for r in range(KN)]
+        values = [val_01[:, 0, :], val_01[:, 1, :], val_2[:], val_3[:]]
+        for weights, product in ((wk_sb, keys), (wv_sb, values)):
             for r in range(KN):
                 looked_up = window[:].indirect(offsets[:, r * (S // 16) : (r + 1) * (S // 16)])
-                nc.tensor.matmul(
-                    product[r * S // BANK][:, r % (BANK // S), :], weights[:], looked_up, start=True, stop=True
-                )
+                nc.tensor.matmul(product[r], weights[:], looked_up, start=True, stop=True)
         prod = held.tile([D, KN, S], BF16, name="prod")
         for b in range(N // BANK):
             ranks = slice(b * BANK // S, (b + 1) * BANK // S)
@@ -110,8 +112,9 @@ def tile_multiscaleknngraphattention_kernel(tc, table, xq, wq, bq, wk, wv, bv, o
         nc.tensor.matmul(idle_ps[:], prod[:, KN - 1, halves[1]], prod[:, KN - 2 : KN, :], start=True, stop=True)
 
         val_sb = held.tile([D, KN, S], F32, name="val_sb")
-        nc.scalar.copy(val_sb[:, 0 : BANK // S, :], val_ps[0][:])
-        nc.vector.tensor_copy(val_sb[:, BANK // S : KN, :], val_ps[1][:])
+        nc.scalar.copy(val_sb[:, 0:2, :], val_01[:])
+        nc.vector.tensor_copy(val_sb[:, 2, :], val_2[:])
+        nc.vector.tensor_copy(val_sb[:, 3, :], val_3[:])
         valT_ps = [bank(f"valT_ps{r}", [P, HALVES, D], F32) for r in range(KN)]
         for r in range(KN):
             for h, nodes in enumerate(halves):

import math

import concourse.mybir as mybir
from concourse.masks import make_identity

S, D, KN, N = 256, 128, 4, 1024
P = 128
BANK = 512
HALVES = S // P
WARM_UP = 7
BF16, F32, U16 = mybir.dt.bfloat16, mybir.dt.float32, mybir.dt.uint16
ACT = mybir.ActivationFunctionType
ALU = mybir.AluOpType
X = mybir.AxisListType.X

FLOPS = 2 * D * D * (S + 2 * N) + 4 * D * N


def tile_multiscaleknngraphattention_kernel(tc, table, xq, wq, bq, wk, wv, bv, offs, out):
    nc = tc.nc
    with tc.tile_pool(name="held", bufs=1) as held, tc.psum_pool(name="banks", bufs=8) as banks:
        def bank(name, shape, dtype):
            return banks.tile(shape, dtype, name=name, tag="bank")

        table_rows = held.tile([P, HALVES, D], BF16, name="table_rows")
        nc.sync.dma_start(table_rows[:], table.rearrange("(h p) d -> p h d", p=P))
        xq_sb = held.tile([D, S], BF16, name="xq_sb")
        nc.sync.dma_start(xq_sb[:], xq)
        wq_sb = held.tile([D, D], BF16, name="wq_sb")
        nc.sync.dma_start(wq_sb[:], wq)
        offsets = held.tile([P, N // 16], U16, name="offsets")
        nc.sync.dma_start(offsets[:], offs)
        wk_sb = held.tile([D, D], BF16, name="wk_sb")
        nc.sync.dma_start(wk_sb[:], wk)
        bq_sb = held.tile([D, 1], F32, name="bq_sb")
        nc.sync.dma_start(bq_sb[:], bq)
        wv_sb = held.tile([D, D], BF16, name="wv_sb")
        nc.sync.dma_start(wv_sb[:], wv)
        bv_sb = held.tile([D, 1], F32, name="bv_sb")
        nc.sync.dma_start(bv_sb[:], bv)

        nothing = held.tile([P, 1], BF16, name="nothing")
        nc.gpsimd.memset(nothing[:], 0.0)
        idle_ps = bank("idle_ps", [P, BANK], F32)
        for i in range(WARM_UP):
            nc.tensor.matmul(
                idle_ps[:, 0 : BANK // 2],
                nothing[:].to_broadcast([P, P]),
                nothing[:].to_broadcast([P, BANK // 2]),
                start=True,
                stop=True,
            )

        identity_bf = held.tile([P, P], BF16, name="identity_bf")
        make_identity(nc, identity_bf[:])
        identity_f = held.tile([P, P], F32, name="identity_f")
        nc.vector.tensor_copy(identity_f[:], identity_bf[:])
        warm = held.tile([P, 1], F32, name="warm")
        nc.vector.memset(warm[:], 0.0)
        nc.scalar.activation(warm[:], warm[:], ACT.Exp)
        same = held.tile([D, KN, KN], BF16, name="same")
        nc.vector.memset(same[:], 0.0)
        for b in range(KN):
            nc.vector.memset(same[:, b, b : b + 1], 1.0)
        signs = held.tile([D, KN, KN, KN], BF16, name="signs")
        nc.vector.tensor_tensor(
            signs[:],
            same[:].unsqueeze(2).to_broadcast([D, KN, KN, KN]),
            same[:].unsqueeze(3).to_broadcast([D, KN, KN, KN]),
            ALU.subtract,
        )

        halves = [slice(h * P, (h + 1) * P) for h in range(HALVES)]

        flipped = bank("flipped", [D, S], BF16)
        for h, nodes in enumerate(halves):
            nc.tensor.transpose(flipped[:, nodes], table_rows[:, h, :], identity_bf[:])
        window = held.tile([D, S], BF16, name="window")
        nc.vector.tensor_copy(window[:], flipped[:])

        q_ps = bank("q_ps", [D, S], F32)
        nc.tensor.matmul(q_ps[:], wq_sb[:], xq_sb[:], start=True, stop=True)
        q_sb = held.tile([D, S], F32, name="q_sb")
        nc.scalar.activation(q_sb[:], q_ps[:], ACT.Identity, bias=bq_sb[:])
        q_twice = q_sb[:].unsqueeze(1).to_broadcast([D, BANK // S, S])

        out_ps = [bank(f"out_ps{h}", [D, P], F32) for h in range(HALVES)]
        for h, nodes in enumerate(halves):
            nc.tensor.matmul(out_ps[h][:], wq_sb[:], xq_sb[:, nodes], start=True, stop=False)

        key_ps = [bank(f"key_ps{b}", [D, BANK // S, S], F32) for b in range(N // BANK)]
        val_01 = bank("val_01", [D, BANK // S, S], F32)
        val_2 = bank("val_2", [D, S], F32)
        val_3 = bank("val_3", [D, S], F32)
        keys = [key_ps[r * S // BANK][:, r % (BANK // S), :] for r in range(KN)]
        values = [val_01[:, 0, :], val_01[:, 1, :], val_2[:], val_3[:]]
        for weights, product in ((wk_sb, keys), (wv_sb, values)):
            for r in range(KN):
                looked_up = window[:].indirect(offsets[:, r * (S // 16) : (r + 1) * (S // 16)])
                nc.tensor.matmul(product[r], weights[:], looked_up, start=True, stop=True)
        prod = held.tile([D, KN, S], BF16, name="prod")
        for b in range(N // BANK):
            ranks = slice(b * BANK // S, (b + 1) * BANK // S)
            nc.vector.tensor_tensor(prod[:, ranks, :], key_ps[b][:], q_twice, ALU.mult)

        diff = bank("diff", [P, HALVES, KN, KN], F32)
        for h, nodes in enumerate(halves):
            for b in range(KN):
                nc.tensor.matmul(diff[:, h], prod[:, b, nodes], signs[:, b], start=(b == 0), stop=(b == KN - 1))

        idle_ps = bank("idle_ps", [P, BANK], F32)
        nc.tensor.matmul(idle_ps[:], prod[:, KN - 1, halves[1]], prod[:, KN - 2 : KN, :], start=True, stop=True)

        val_sb = held.tile([D, KN, S], F32, name="val_sb")
        nc.scalar.copy(val_sb[:, 0:2, :], val_01[:])
        nc.vector.tensor_copy(val_sb[:, 2, :], val_2[:])
        nc.vector.tensor_copy(val_sb[:, 3, :], val_3[:])
        valT_ps = [bank(f"valT_ps{r}", [P, HALVES, D], F32) for r in range(KN)]
        for r in range(KN):
            for h, nodes in enumerate(halves):
                nc.tensor.transpose(valT_ps[r][:, h, :], val_sb[:, r, nodes], identity_f[:])

        nc.tensor.matmul(idle_ps[:, 0:P], identity_f[:], val_sb[:, KN - 1, halves[1]], start=True, stop=True)

        e = held.tile([P, HALVES * KN, KN], F32, name="e")
        nc.scalar.activation(e[:], diff[:].rearrange("p h r x -> p (h r) x"), ACT.Exp, scale=1.0 / math.sqrt(D))
        total = held.tile([P, HALVES * KN], F32, name="total")
        nc.vector.tensor_reduce(total[:], e[:], X, ALU.add)
        a = held.tile([P, HALVES * KN], F32, name="a")
        nc.vector.reciprocal(a[:], total[:])

        scaled = held.tile([P, KN, HALVES, D], F32, name="scaled")
        for k in range(KN // 2):
            for h in range(HALVES):
                for r in (2 * k, 2 * k + 1):
                    column = a[:, h * KN + r : h * KN + r + 1]
                    if r % 2 == 0:
                        nc.vector.tensor_scalar(scaled[:, r, h, :], valT_ps[r][:, h, :], column, None, ALU.mult)
                    else:
                        nc.scalar.activation(scaled[:, r, h, :], valT_ps[r][:, h, :], ACT.Copy, scale=column)
                    nc.tensor.matmul(
                        out_ps[h][:], scaled[:, r, h, :], identity_f[:], is_transpose=True, start=False, stop=(r == KN - 1)
                    )

        bias_out = held.tile([D, 1], F32, name="bias_out")
        nc.gpsimd.tensor_tensor(bias_out[:], bq_sb[:], bv_sb[:], ALU.add)
        result = held.tile([D, S], F32, name="result")
        nc.vector.tensor_scalar(result[:, halves[0]], out_ps[0][:], bias_out[:], None, ALU.add)
        nc.sync.dma_start(out[:, halves[0]], result[:, halves[0]])
        nc.scalar.activation(result[:, halves[1]], out_ps[1][:], ACT.Identity, bias=bias_out[:])
        nc.sync.dma_start(out[:, halves[1]], result[:, halves[1]])
